import numpy as np
import ml_dtypes


def mxq(x, axis, fmt="e4m3"):
    dtype, down = {"e4m3": (ml_dtypes.float8_e4m3fn, 7), "e5m2": (ml_dtypes.float8_e5m2, 14)}[fmt]
    v = np.moveaxis(np.asarray(x, np.float32).astype(ml_dtypes.bfloat16).astype(np.float64), axis, -1)
    blocks = v.reshape(v.shape[:-1] + (-1, 32))
    amax = np.abs(blocks).max(-1, keepdims=True)
    byte = np.maximum(np.where(amax > 0, np.frexp(amax)[1] - 1 + 127, 0) - down, 1)
    scale = np.exp2(byte - 127.0)
    codes = (blocks / scale).astype(np.float32).astype(dtype).astype(np.float64)
    return np.moveaxis((codes * scale).reshape(v.shape), -1, axis)


WIDE = False


def mx_kscale(k):
    if not WIDE:
        return np.ones(k)
    levels = np.array([10, -10, 5, -5, 0])
    if k % 512:
        return np.exp2(np.random.permutation(np.resize(levels, k // 32))).repeat(32)
    a = np.empty((k // 512, 16))
    for p in range(k // 512):
        a[p, :8] = np.random.permutation(np.resize(levels, 8))
        for g in range(8):
            far = levels[np.abs(levels - a[p, g]) >= 10]
            a[p, g + 8] = far[np.random.randint(len(far))]
    return np.exp2(a.ravel()).repeat(32)


BF16 = ml_dtypes.bfloat16


def bf(x):
    return np.asarray(x, np.float32).astype(BF16)


def f64(x):
    return np.asarray(x).astype(np.float64)


B, T, I, H = 128, 8, 1024, 1024


def sigmoid(v):
    return 1.0 / (1.0 + np.exp(-v))


def draw0():
    s = mx_kscale(I)
    d = {"inputs": bf(np.random.standard_normal((B, T, I)) * s),
         "h0": bf(np.random.standard_normal((1, B, H))),
         "c0": bf(np.random.standard_normal((1, B, H)))}
    for ni, nh in (("ii", "hi"), ("if_", "hf"), ("io", "ho"), ("ig", "hg")):
        d["w_" + ni] = bf(np.random.standard_normal((H, I)) / np.sqrt(I) / s[None, :])
        d["b_" + ni] = bf(np.random.standard_normal((H, 1)) * 0.3)
        d["w_" + nh] = bf(np.random.standard_normal((H, H)) * 0.7 / np.sqrt(H))
        d["b_" + nh] = bf(np.random.standard_normal((H, 1)) * 0.3)
    return d


def core(inputs, h0, c0, w_ii, b_ii, w_hi, b_hi, w_if_, b_if_, w_hf, b_hf, w_io, b_io, w_ho, b_ho, w_ig, b_ig, w_hg, b_hg):
    xq = mxq(f64(inputs), 2, "e4m3")
    h0s = f64(h0)[0]
    c0s = f64(c0)[0]
    zi = (xq @ mxq(f64(w_ii), 1, "e4m3").T) + (h0s @ f64(w_hi).T)[:, None, :] + f64(b_ii)[:, 0] + f64(b_hi)[:, 0]
    zf = (xq @ mxq(f64(w_if_), 1, "e4m3").T) + (h0s @ f64(w_hf).T)[:, None, :] + f64(b_if_)[:, 0] + f64(b_hf)[:, 0]
    zg = (xq @ mxq(f64(w_ig), 1, "e4m3").T) + (h0s @ f64(w_hg).T)[:, None, :] + f64(b_ig)[:, 0] + f64(b_hg)[:, 0]
    zo = (xq @ mxq(f64(w_io), 1, "e4m3").T) + (h0s @ f64(w_ho).T)[:, None, :] + f64(b_io)[:, 0] + f64(b_ho)[:, 0]
    i = sigmoid(zi)
    f = sigmoid(zf)
    g = np.tanh(zg)
    o = sigmoid(zo)
    c_next = f * c0s[:, None, :] + i * g
    h_next = o * np.tanh(c_next)
    hidden_seq = np.transpose(h_next, (1, 0, 2))
    h_last = hidden_seq[-1][None]
    c_last = c_next[:, -1][None]
    return hidden_seq, h_last, c_last


def e4m3fn_bytes(y):
    return np.clip(np.asarray(y, np.float64), -448.0, 448.0).astype(np.float32).astype(ml_dtypes.float8_e4m3fn).view(np.uint8)


def e4m3fn_values(b):
    return np.asarray(b, np.uint8).view(ml_dtypes.float8_e4m3fn).astype(np.float64)


def setup_inputs():
    d = draw0()
    x0 = np.asarray(d['w_io']).astype(np.float64)
    s = (np.max(np.abs(x0), axis=(0,), keepdims=True) / 448.0).astype(np.float32)
    out = {}
    for k, v in d.items():
        if k == 'w_io':
            out['w_io_bytes'] = e4m3fn_bytes(x0 / s.astype(np.float64))
            out['w_io_scale'] = s
        else:
            out[k] = v
    return out


def reference(inputs, h0, c0, w_ii, b_ii, w_hi, b_hi, w_if_, b_if_, w_hf, b_hf, w_io_bytes, w_io_scale, b_io, w_ho, b_ho, w_ig, b_ig, w_hg, b_hg):
    return core(inputs, h0, c0, w_ii, b_ii, w_hi, b_hi, w_if_, b_if_, w_hf, b_hf, e4m3fn_values(w_io_bytes) * w_io_scale.astype(np.float64), b_io, w_ho, b_ho, w_ig, b_ig, w_hg, b_hg)

@@ -1,0 +1,433 @@
+from contextlib import ExitStack
+
+import concourse.mybir as mybir
+from concourse.masks import make_identity
+
+F32 = mybir.dt.float32
+BF16 = mybir.dt.bfloat16
+U32 = mybir.dt.uint32
+U8 = mybir.dt.uint8
+FP8 = mybir.dt.float8_e4m3fn
+FP8X4 = mybir.dt.float8_e4m3fn_x4
+ACT = mybir.ActivationFunctionType
+ALU = mybir.AluOpType
+
+B, T, I, H = 128, 8, 1024, 1024
+P = 128
+FLOPS = 2 * B * T * I * 4 * H + 2 * B * H * 4 * H
+
+SIZES = [256, 256, 256, 256]
+WORDS_H = True
+RB = 5
+ORDER_A = False
+RAMPMIX = False
+LI = 2
+QPOS = 4
+EV_TH = "ss"
+EV_TI = "ss"
+EV_HB = "v"
+E_IG = "vgvg"
+E_FC = "vgvg"
+E_C = "gggg"
+E_H = "vgvg"
+T_FC = "vvvv"
+T_C = "vgvg"
+T_H = "vvvv"
+T_H2 = "ggvv"
+WEARLY = 4
+
+
+def tile_naivelstm_pa_kernel(
+    tc, inputs, h0, c0, w_ii, b_ii, w_hi, b_hi, w_if_, b_if_, w_hf, b_hf,
+    w_io_bytes, w_io_scale, b_io, w_ho, b_ho, w_ig, b_ig, w_hg, b_hg,
+    out_0, out_1, out_2,
+):
+    nc = tc.nc
+    w_in = [w_ii, w_ig, w_if_, None]
+    w_hid = [w_hi, w_hg, w_hf, w_ho]
+    b_in = [b_ii, b_ig, b_if_, b_io]
+    b_hid = [b_hi, b_hg, b_hf, b_ho]
+    funcs = [ACT.Sigmoid, ACT.Tanh, ACT.Sigmoid, ACT.Sigmoid]
+    starts = [sum(SIZES[:i]) for i in range(len(SIZES))]
+    NCH = len(SIZES)
+    NSTEP = 4 * NCH
+    STEPS = [(c, q) for c in range(NCH - 2) for q in range(4)]
+    STEPS += [(c, q) for c in (NCH - 2, NCH - 1) for q in range(3)] + [(NCH - 2, 3), (NCH - 1, 3)]
+    f_at = dict((c, STEPS.index((c, 2))) for c in range(NCH))
+
+    def geo(c):
+        size = SIZES[c]
+        return starts[c], size, size // P, 512 // size, T * size // 512
+
+    with ExitStack() as ctx:
+        ctx.enter_context(tc.manual_schedule())
+        const = ctx.enter_context(tc.tile_pool(name="const", bufs=1))
+        raw = ctx.enter_context(tc.tile_pool(name="raw", bufs=RB))
+        stage = ctx.enter_context(tc.tile_pool(name="stage", bufs=3))
+        zp = ctx.enter_context(tc.tile_pool(name="zp", bufs=2))
+        psum = ctx.enter_context(tc.psum_pool(name="psum", bufs=8))
+
+        ident_f = const.tile([P, P], F32, name="ident_f")
+        ident_b = const.tile([P, P], BF16, name="ident_b")
+        ones_b = const.tile([P, P], BF16, name="ones_b")
+        warm = const.tile([P, 1], F32, name="warm")
+        bias_rows = const.tile([P, 4, H], BF16, name="bias_rows")
+        scale_bc = const.tile([P, I], F32, name="scale_bc")
+        x_sb = const.tile([P, T, I], BF16, name="x_sb")
+        h0_sb = const.tile([P, H], BF16, name="h0_sb")
+        c0_sb = const.tile([P, H], BF16, name="c0_sb")
+        h0T = const.tile([P, 8, P], BF16, name="h0T")
+        x_codes = const.tile([P, T, 2 * P], U32, name="x_codes", align_bytes=64)
+        x_scales = const.tile([P, T, 2 * P], U8, name="x_scales", align_bytes=64)
+
+        st = {}
+
+        def evac(eng, out, in_):
+            if eng == "v":
+                nc.vector.tensor_copy(out=out, in_=in_)
+            else:
+                nc.scalar.copy(out=out, in_=in_)
+
+        def load(s):
+            if s >= NSTEP:
+                return
+            c, q = STEPS[s]
+            u0, size, nj, tpb, nb = geo(c)
+            rows = slice(u0, u0 + size)
+            wh_raw = raw.tile([P, nj, H], BF16, name="wh_raw", tag="wh_raw")
+            nc.sync.dma_start(out=wh_raw[:], in_=w_hid[q][rows, :].rearrange("(j p) k -> p j k", p=P))
+            st[("wh_raw", s)] = wh_raw
+            if q == 3:
+                wbytes = raw.tile([P, nj, I], U8, name="wbytes", tag="wbytes", bufs=2)
+                nc.sync.dma_start(out=wbytes[:], in_=w_io_bytes[rows, :].rearrange("(j p) k -> p j k", p=P))
+                st[("wbytes", s)] = wbytes
+                w_wide = raw.tile([P, nj, I], BF16, name="w_wide", tag="w_wide", bufs=2)
+                st[("w_raw", s)] = w_wide
+            else:
+                w_raw = raw.tile([P, nj, I], BF16, name="w_raw", tag="w_raw")
+                nc.sync.dma_start(out=w_raw[:], in_=w_in[q][rows, :].rearrange("(j p) k -> p j k", p=P))
+                st[("w_raw", s)] = w_raw
+
+        def widen(s):
+            if s >= NSTEP:
+                return
+            for j in range(geo(STEPS[s][0])[2]):
+                nc.vector.tensor_tensor(
+                    out=st[("w_raw", s)][:, j, :],
+                    in0=st[("wbytes", s)][:, j, :].bitcast(FP8),
+                    in1=scale_bc[:],
+                    op=ALU.mult,
+                )
+
+        def word_transposes(src_row, step):
+            words = src_row.bitcast(F32)
+            tr = psum.tile([P, 512], F32, name="tr", tag="bank")
+            for a in range(4):
+                if step == 2:
+                    src = words[:, 256 * (a // 2) + a % 2:256 * (a // 2 + 1):2]
+                else:
+                    src = words[:, a * P:(a + 1) * P]
+                nc.tensor.transpose(tr[:, a * P:(a + 1) * P], src, ident_f[:])
+            return tr
+
+        def tx(tp, engs):
+            xg = stage.tile([P, 2, 1024], BF16, name="xg", tag="grp", align_bytes=64)
+            st[("xg", tp)] = xg
+            for tt in range(2):
+                tr = word_transposes(x_sb[:, 2 * tp + tt, :], 2)
+                evac(
+                    engs[tt],
+                    xg[:, tt, :].bitcast(F32).rearrange("p (g b u) -> p g b u", g=2, u=2),
+                    tr[:].rearrange("p (g u b) -> p g b u", g=2, u=2),
+                )
+
+        def qx(tp):
+            nc.vector.quantize_mx(
+                out=x_codes[:, 2 * tp:2 * tp + 2, :].rearrange("p t w -> p (t w)").bitcast(FP8X4),
+                scales=x_scales[:, 2 * tp:2 * tp + 2, :].rearrange("p t w -> p (t w)"),
+                in_=st[("xg", tp)][:].rearrange("p a k -> p (a k)"),
+            )
+
+        def ti(s, engs):
+            if s >= NSTEP:
+                return
+            u0, size, nj, tpb, nb = geo(STEPS[s][0])
+            wg = stage.tile([P, 8 * size], BF16, name="wg", tag="grp", align_bytes=64)
+            st[("wg", s)] = wg
+            for j in range(nj):
+                tr = word_transposes(st[("w_raw", s)][:, j, :], 2)
+                evac(
+                    engs[j],
+                    wg[:].bitcast(F32).rearrange("p (g r u) -> p g r u", g=2, u=2)[:, :, j * P:(j + 1) * P, :],
+                    tr[:].rearrange("p (g u r) -> p g r u", g=2, u=2),
+                )
+
+        def qw(s):
+            if s >= NSTEP:
+                return
+            size = geo(STEPS[s][0])[1]
+            w_codes = stage.tile([P, 2 * size], U32, name="w_codes", tag="w_codes", align_bytes=64)
+            w_scales = stage.tile([P, 2 * size], U8, name="w_scales", tag="w_scales", align_bytes=64)
+            st[("w_codes", s)] = w_codes
+            st[("w_scales", s)] = w_scales
+            nc.vector.quantize_mx(out=w_codes[:].bitcast(FP8X4), scales=w_scales[:], in_=st[("wg", s)][:])
+
+        def bf_transposes(src_row):
+            trb = psum.tile([P, 1024], BF16, name="trb", tag="bank")
+            for k in range(8):
+                nc.tensor.transpose(trb[:, k * P:(k + 1) * P], src_row[:, k * P:(k + 1) * P], ident_b[:])
+            return trb
+
+        def th0():
+            if WORDS_H:
+                tr = word_transposes(h0_sb, 1)
+                nc.vector.tensor_copy(
+                    out=h0T[:].rearrange("p (a e) b -> p a e b", e=2),
+                    in_=tr[:].bitcast(BF16).rearrange("p (a b e) -> p a e b", a=4, e=2),
+                )
+            else:
+                trb = bf_transposes(h0_sb)
+                evac("s", h0T[:].rearrange("p k b -> p (k b)"), trb[:])
+
+        def th(s, engs):
+            if s >= NSTEP:
+                return
+            u0, size, nj, tpb, nb = geo(STEPS[s][0])
+            if WORDS_H:
+                whT = stage.tile([P, 4, size], F32, name="whT", tag="whT")
+            else:
+                whT = stage.tile([P, 8, size], BF16, name="whT", tag="whT")
+            st[("whT", s)] = whT
+            for j in range(nj):
+                if WORDS_H:
+                    tr = word_transposes(st[("wh_raw", s)][:, j, :], 1)
+                    evac(engs[j], whT[:, :, j * P:(j + 1) * P], tr[:].rearrange("p (a r) -> p a r", a=4))
+                else:
+                    trb = bf_transposes(st[("wh_raw", s)][:, j, :])
+                    evac(engs[j], whT[:, :, j * P:(j + 1) * P], trb[:].rearrange("p (k r) -> p k r", k=8))
+
+        def hm(s, eng):
+            if s >= NSTEP:
+                return
+            c, q = STEPS[s]
+            u0, size, nj, tpb, nb = geo(c)
+            hb_ps = psum.tile([P, size], F32, name="hb_ps", tag="bank")
+            whT = st[("whT", s)]
+            for k in range(8):
+                if WORDS_H:
+                    rhs = whT[:, k // 2, :].bitcast(BF16)[:, k % 2::2]
+                else:
+                    rhs = whT[:, k, :]
+                nc.tensor.matmul(out=hb_ps[:], lhsT=h0T[:, k, :], rhs=rhs, start=(k == 0), stop=False)
+            nc.tensor.matmul(out=hb_ps[:], lhsT=ones_b[:], rhs=bias_rows[:, q, u0:u0 + size], start=False, stop=True)
+            hb_sb = stage.tile([P, size], F32, name="hb_sb", tag="hb_sb")
+            st[("hb", s)] = hb_sb
+            evac(eng, hb_sb[:], hb_ps[:])
+
+        def mx(s, b):
+            u0, size, nj, tpb, nb = geo(STEPS[s][0])
+            acc = psum.tile([P, tpb, size], F32, name="acc", tag="bank")
+            st[("acc", s, b)] = acc
+            w_codes = st[("w_codes", s)]
+            w_scales = st[("w_scales", s)]
+            for tt in range(tpb):
+                t = tpb * b + tt
+                for g in range(2):
+                    nc.tensor.matmul_mx(
+                        out=acc[:, tt, :],
+                        lhsT=x_codes[:, t, g * P:(g + 1) * P].bitcast(FP8X4),
+                        lhsT_scale=x_scales[:, t, g * P:(g + 1) * P],
+                        rhs=w_codes[:, g * size:(g + 1) * size].bitcast(FP8X4),
+                        rhs_scale=w_scales[:, g * size:(g + 1) * size],
+                        start=(g == 0),
+                        stop=(g == 1),
+                    )
+
+        def piece(c, q, b):
+            tpb = geo(c)[3]
+            return st[("z", c, q)][:, b * tpb:(b + 1) * tpb, :]
+
+        def add(s, b):
+            c, q = STEPS[s]
+            u0, size, nj, tpb, nb = geo(c)
+            nc.vector.tensor_tensor(
+                out=piece(c, q, b),
+                in0=st[("acc", s, b)][:],
+                in1=st[("hb", s)][:].unsqueeze(1).to_broadcast([P, tpb, size]),
+                op=ALU.add,
+            )
+
+        def actv(s, b0, b1):
+            c, q = STEPS[s]
+            tpb = geo(c)[3]
+            z = st[("z", c, q)][:, b0 * tpb:b1 * tpb, :]
+            nc.scalar.activation(out=z, in_=z, func=funcs[q])
+
+        def tt_on(eng, out, in0, in1, op):
+            if eng == "v":
+                nc.vector.tensor_tensor(out=out, in0=in0, in1=in1, op=op)
+            else:
+                nc.gpsimd.tensor_tensor(out=out, in0=in0, in1=in1, op=op)
+
+        def p_ig(c, b, eng):
+            tt_on(eng, piece(c, 0, b), piece(c, 0, b), piece(c, 1, b), ALU.mult)
+
+        def p_fc(c, b, eng):
+            u0, size, nj, tpb, nb = geo(c)
+            tt_on(eng, piece(c, 2, b), piece(c, 2, b),
+                  c0_sb[:, u0:u0 + size].unsqueeze(1).to_broadcast([P, tpb, size]), ALU.mult)
+
+        def p_c(c, b, eng):
+            u0, size, nj, tpb, nb = geo(c)
+            tt_on(eng, piece(c, 2, b), piece(c, 2, b), piece(c, 0, b), ALU.add)
+            if b == nb - 1:
+                nc.sync.dma_start(out=out_2[0, :, u0:u0 + size], in_=st[("z", c, 2)][:, T - 1, :])
+
+        def tanh_c(c, b):
+            nc.scalar.activation(out=piece(c, 1, b), in_=piece(c, 2, b), func=ACT.Tanh)
+
+        def p_h(c, b, eng):
+            u0, size, nj, tpb, nb = geo(c)
+            tt_on(eng, piece(c, 3, b), piece(c, 3, b), piece(c, 1, b), ALU.mult)
+            nc.sync.dma_start(
+                out=out_0[b * tpb:(b + 1) * tpb, :, u0:u0 + size].rearrange("t b h -> b t h"), in_=piece(c, 3, b)
+            )
+            if b == nb - 1:
+                nc.sync.dma_start(out=out_1[0, :, u0:u0 + size], in_=st[("z", c, 3)][:, T - 1, :])
+
+        nc.vector.memset(warm[:], 0.0)
+        nc.scalar.activation(out=warm[:], in_=warm[:], func=ACT.Sigmoid)
+        if not WORDS_H:
+            make_identity(nc, ident_b[:])
+        make_identity(nc, ident_f[:])
+        nc.vector.memset(ones_b[:], 1.0)
+        nc.vector.memset(bias_rows[:], 0.0)
+        nc.sync.dma_start(out=h0_sb[:], in_=h0[0])
+        load(0)
+        for tp in range(4):
+            nc.sync.dma_start(out=x_sb[:, 2 * tp:2 * tp + 2, :], in_=inputs[:, 2 * tp:2 * tp + 2, :])
+        for q in range(4):
+            nc.scalar.dma_start(out=bias_rows[0:1, q, :], in_=b_in[q].rearrange("n o -> o n"))
+            nc.scalar.dma_start(out=bias_rows[1:2, q, :], in_=b_hid[q].rearrange("n o -> o n"))
+        load(1)
+        load(2)
+        nc.sync.dma_start(out=scale_bc[:], in_=w_io_scale.rearrange("o k -> (o k)").partition_broadcast(P))
+        load(3)
+        nc.sync.dma_start(out=c0_sb[:], in_=c0[0])
+        for s in range(4, RB):
+            load(s)
+
+        th0()
+        th(0, "vs")
+        ti(0, "vs")
+        tx(0, "vs")
+        qw(0)
+        if RAMPMIX:
+            st[("z", 0, 0)] = zp.tile([P, T, SIZES[0]], F32, name="z0", tag="z0")
+            hm(0, "v")
+            tx(1, "vs")
+            qx(0)
+            tx(2, "vs")
+            qx(1)
+            mx(0, 0)
+            tx(3, "vs")
+            qx(2)
+            add(0, 0)
+            mx(0, 1)
+            th(1, "vs")
+            qx(3)
+            add(0, 1)
+            actv(0, 0, 2)
+            mx(0, 2)
+            ti(1, "vs")
+            add(0, 2)
+            mx(0, 3)
+            add(0, 3)
+            actv(0, 2, 4)
+        else:
+            tx(1, "vs")
+            hm(0, "v")
+            qx(0)
+            tx(2, "vs")
+            qx(1)
+            tx(3, "vs")
+            qx(2)
+            th(1, "vs")
+            qx(3)
+            ti(1, "vs")
+        if LI == 3:
+            qw(1)
+            ti(2, "vs")
+            widen(3)
+        load(RB)
+        load(RB + 1)
+
+        def late(c, half):
+            nb = geo(c)[4]
+            return range(half * nb // 2, (half + 1) * nb // 2)
+
+        for s in range(NSTEP - 2):
+            c, q = STEPS[s]
+            u0, size, nj, tpb, nb = geo(c)
+            st[("z", c, q)] = zp.tile([P, T, size], F32, name="z%d" % q, tag="z%d" % q)
+            due = [(cc, s - f_at[cc] - 2) for cc in range(NCH) if s - f_at[cc] in (2, 3)]
+            for cc, h in due:
+                for b in late(cc, h):
+                    tanh_c(cc, b)
+            for b in range(nb):
+                mx(s, b)
+            for b in range(nb):
+                add(s, b)
+                if b == nb // 2 - 1:
+                    actv(s, 0, nb // 2)
+            actv(s, nb // 2, nb)
+            qw(s + 1)
+            hm(s + 1, EV_HB)
+            for cc, h in due:
+                if cc < NCH - 2:
+                    for b in late(cc, h):
+                        p_h(cc, b, E_H[b])
+            last_f = s == NSTEP - 3
+            if q == 1:
+                for b in range(nb):
+                    p_ig(c, b, E_IG[b])
+            if q == 2:
+                for a in range(0, nb, 2):
+                    p_fc(c, a, (T_FC if last_f else E_FC)[a])
+                    p_fc(c, a + 1, (T_FC if last_f else E_FC)[a + 1])
+                    p_c(c, a, (T_C if last_f else E_C)[a])
+                    p_c(c, a + 1, (T_C if last_f else E_C)[a + 1])
+            th(s + 2, EV_TH)
+            for so in range(NSTEP):
+                if STEPS[so][1] == 3 and s == (so - 3 if so < NSTEP - 2 else so - WEARLY):
+                    widen(so)
+            ti(s + 2, EV_TI)
+            load(s + 2 + RB)
+
+        sa, sb = NSTEP - 2, NSTEP - 1
+        ca, cb = NCH - 2, NCH - 1
+        nb = geo(cb)[4]
+        for s in (sa, sb):
+            st[("z", STEPS[s][0], 3)] = zp.tile([P, T, geo(STEPS[s][0])[1]], F32, name="z3", tag="z3")
+        for b in range(nb):
+            mx(sa, b)
+        hm(sb, "s")
+        for b in range(nb):
+            add(sa, b)
+            if b == 0:
+                qw(sb)
+            actv(sa, b, b + 1)
+            if b % 2 == 1:
+                tanh_c(cb, b - 1)
+                tanh_c(cb, b)
+            if T_H2[b] == "g":
+                p_h(ca, b, "g")
+        for b in range(nb):
+            mx(sb, b)
+        for b in range(nb):
+            add(sb, b)
+            actv(sb, b, b + 1)
+            if T_H2[b] == "v":
+                p_h(ca, b, "v")
+        for b in range(nb):
+            p_h(cb, b, T_H[b])

@@ -34,6 +34,9 @@ T_FC = "vvvv"
 T_C = "vgvg"
 T_H = "vvvv"
 T_H2 = "ggvv"
+IDLE = [6, 0]
+F2 = (1, 1)
+R_EV = "ss"
 WEARLY = 4
 
 
@@ -70,6 +73,7 @@ def tile_naivelstm_pa_kernel(
         ident_f = const.tile([P, P], F32, name="ident_f")
         ident_b = const.tile([P, P], BF16, name="ident_b")
         ones_b = const.tile([P, P], BF16, name="ones_b")
+        zeros_b = const.tile([P, 512], BF16, name="zeros_b")
         warm = const.tile([P, 1], F32, name="warm")
         bias_rows = const.tile([P, 4, H], BF16, name="bias_rows")
         scale_bc = const.tile([P, I], F32, name="scale_bc")
@@ -89,6 +93,20 @@ def tile_naivelstm_pa_kernel(
                 nc.scalar.copy(out=out, in_=in_)
 
         def load(s):
+            load_wh(s)
+            load_w(s)
+
+        def load_bias(q):
+            nc.sync.dma_start(out=bias_rows[0:1, q, :], in_=b_in[q].rearrange("n o -> o n"))
+            nc.sync.dma_start(out=bias_rows[1:2, q, :], in_=b_hid[q].rearrange("n o -> o n"))
+
+        def idle(n):
+            if n:
+                idle_ps = psum.tile([P, 512], F32, name="idle_ps", tag="bank")
+                for i in range(n):
+                    nc.tensor.matmul(out=idle_ps[:], lhsT=ones_b[:], rhs=zeros_b[:], start=True, stop=True)
+
+        def load_wh(s):
             if s >= NSTEP:
                 return
             c, q = STEPS[s]
@@ -97,6 +115,13 @@ def tile_naivelstm_pa_kernel(
             wh_raw = raw.tile([P, nj, H], BF16, name="wh_raw", tag="wh_raw")
             nc.sync.dma_start(out=wh_raw[:], in_=w_hid[q][rows, :].rearrange("(j p) k -> p j k", p=P))
             st[("wh_raw", s)] = wh_raw
+
+        def load_w(s):
+            if s >= NSTEP:
+                return
+            c, q = STEPS[s]
+            u0, size, nj, tpb, nb = geo(c)
+            rows = slice(u0, u0 + size)
             if q == 3:
                 wbytes = raw.tile([P, nj, I], U8, name="wbytes", tag="wbytes", bufs=2)
                 nc.sync.dma_start(out=wbytes[:], in_=w_io_bytes[rows, :].rearrange("(j p) k -> p j k", p=P))
@@ -119,9 +144,11 @@ def tile_naivelstm_pa_kernel(
                     op=ALU.mult,
                 )
 
-        def word_transposes(src_row, step):
+        def word_transposes(src_row, step, fill=0):
             words = src_row.bitcast(F32)
             tr = psum.tile([P, 512], F32, name="tr", tag="bank")
+            for i in range(fill):
+                nc.tensor.matmul(out=tr[:], lhsT=ones_b[:], rhs=zeros_b[:], start=True, stop=True)
             for a in range(4):
                 if step == 2:
                     src = words[:, 256 * (a // 2) + a % 2:256 * (a // 2 + 1):2]
@@ -130,11 +157,11 @@ def tile_naivelstm_pa_kernel(
                 nc.tensor.transpose(tr[:, a * P:(a + 1) * P], src, ident_f[:])
             return tr
 
-        def tx(tp, engs):
+        def tx(tp, engs, fill=(0, 0)):
             xg = stage.tile([P, 2, 1024], BF16, name="xg", tag="grp", align_bytes=64)
             st[("xg", tp)] = xg
             for tt in range(2):
-                tr = word_transposes(x_sb[:, 2 * tp + tt, :], 2)
+                tr = word_transposes(x_sb[:, 2 * tp + tt, :], 2, fill[tt])
                 evac(
                     engs[tt],
                     xg[:, tt, :].bitcast(F32).rearrange("p (g b u) -> p g b u", g=2, u=2),
@@ -148,14 +175,14 @@ def tile_naivelstm_pa_kernel(
                 in_=st[("xg", tp)][:].rearrange("p a k -> p (a k)"),
             )
 
-        def ti(s, engs):
+        def ti(s, engs, fill=(0, 0)):
             if s >= NSTEP:
                 return
             u0, size, nj, tpb, nb = geo(STEPS[s][0])
             wg = stage.tile([P, 8 * size], BF16, name="wg", tag="grp", align_bytes=64)
             st[("wg", s)] = wg
             for j in range(nj):
-                tr = word_transposes(st[("w_raw", s)][:, j, :], 2)
+                tr = word_transposes(st[("w_raw", s)][:, j, :], 2, fill[j])
                 evac(
                     engs[j],
                     wg[:].bitcast(F32).rearrange("p (g r u) -> p g r u", g=2, u=2)[:, :, j * P:(j + 1) * P, :],
@@ -178,18 +205,19 @@ def tile_naivelstm_pa_kernel(
                 nc.tensor.transpose(trb[:, k * P:(k + 1) * P], src_row[:, k * P:(k + 1) * P], ident_b[:])
             return trb
 
-        def th0():
+        def th0(fill=0):
             if WORDS_H:
-                tr = word_transposes(h0_sb, 1)
-                nc.vector.tensor_copy(
-                    out=h0T[:].rearrange("p (a e) b -> p a e b", e=2),
-                    in_=tr[:].bitcast(BF16).rearrange("p (a b e) -> p a e b", a=4, e=2),
+                tr = word_transposes(h0_sb, 1, fill)
+                evac(
+                    "s",
+                    h0T[:].rearrange("p (a e) b -> p a e b", e=2),
+                    tr[:].bitcast(BF16).rearrange("p (a b e) -> p a e b", a=4, e=2),
                 )
             else:
                 trb = bf_transposes(h0_sb)
                 evac("s", h0T[:].rearrange("p k b -> p (k b)"), trb[:])
 
-        def th(s, engs):
+        def th(s, engs, fill=(0, 0)):
             if s >= NSTEP:
                 return
             u0, size, nj, tpb, nb = geo(STEPS[s][0])
@@ -200,7 +228,7 @@ def tile_naivelstm_pa_kernel(
             st[("whT", s)] = whT
             for j in range(nj):
                 if WORDS_H:
-                    tr = word_transposes(st[("wh_raw", s)][:, j, :], 1)
+                    tr = word_transposes(st[("wh_raw", s)][:, j, :], 1, fill[j])
                     evac(engs[j], whT[:, :, j * P:(j + 1) * P], tr[:].rearrange("p (a r) -> p a r", a=4))
                 else:
                     trb = bf_transposes(st[("wh_raw", s)][:, j, :])
@@ -297,76 +325,69 @@ def tile_naivelstm_pa_kernel(
 
         nc.vector.memset(warm[:], 0.0)
         nc.scalar.activation(out=warm[:], in_=warm[:], func=ACT.Sigmoid)
-        if not WORDS_H:
-            make_identity(nc, ident_b[:])
-        make_identity(nc, ident_f[:])
         nc.vector.memset(ones_b[:], 1.0)
+        nc.vector.memset(zeros_b[:], 0.0)
+        make_identity(nc, ident_f[:])
         nc.vector.memset(bias_rows[:], 0.0)
+        load_w(0)
+        nc.sync.dma_start(out=x_sb[:, 0:2, :], in_=inputs[:, 0:2, :])
         nc.sync.dma_start(out=h0_sb[:], in_=h0[0])
-        load(0)
-        for tp in range(4):
+        load_wh(0)
+        load_bias(0)
+        for tp in range(1, 4):
             nc.sync.dma_start(out=x_sb[:, 2 * tp:2 * tp + 2, :], in_=inputs[:, 2 * tp:2 * tp + 2, :])
-        for q in range(4):
-            nc.scalar.dma_start(out=bias_rows[0:1, q, :], in_=b_in[q].rearrange("n o -> o n"))
-            nc.scalar.dma_start(out=bias_rows[1:2, q, :], in_=b_hid[q].rearrange("n o -> o n"))
         load(1)
+        load_bias(1)
         load(2)
+        load_bias(2)
         nc.sync.dma_start(out=scale_bc[:], in_=w_io_scale.rearrange("o k -> (o k)").partition_broadcast(P))
         load(3)
+        load_bias(3)
         nc.sync.dma_start(out=c0_sb[:], in_=c0[0])
         for s in range(4, RB):
             load(s)
 
-        th0()
-        th(0, "vs")
-        ti(0, "vs")
-        tx(0, "vs")
+        st[("z", 0, 0)] = zp.tile([P, T, SIZES[0]], F32, name="z0", tag="z0")
+        idle(IDLE[0])
+        ti(0, "vs", F2)
+        tx(0, "ss", F2)
         qw(0)
-        if RAMPMIX:
-            st[("z", 0, 0)] = zp.tile([P, T, SIZES[0]], F32, name="z0", tag="z0")
-            hm(0, "v")
-            tx(1, "vs")
-            qx(0)
-            tx(2, "vs")
-            qx(1)
-            mx(0, 0)
-            tx(3, "vs")
-            qx(2)
-            add(0, 0)
-            mx(0, 1)
-            th(1, "vs")
-            qx(3)
-            add(0, 1)
-            actv(0, 0, 2)
-            mx(0, 2)
-            ti(1, "vs")
-            add(0, 2)
-            mx(0, 3)
-            add(0, 3)
-            actv(0, 2, 4)
-        else:
-            tx(1, "vs")
-            hm(0, "v")
-            qx(0)
-            tx(2, "vs")
-            qx(1)
-            tx(3, "vs")
-            qx(2)
-            th(1, "vs")
-            qx(3)
-            ti(1, "vs")
-        if LI == 3:
-            qw(1)
-            ti(2, "vs")
-            widen(3)
+        th0(F2[0])
+        th(0, "vs", F2)
+        qx(0)
+        tx(1, "vs", F2)
+        mx(0, 0)
+        tx(2, "ss")
+        qx(1)
+        hm(0, "v")
+        tx(3, "vs")
+        add(0, 0)
+        mx(0, 1)
+        qx(2)
+        th(1, "ss")
+        add(0, 1)
+        mx(0, 2)
+        qx(3)
+        actv(0, 0, 2)
+        ti(1, "vs")
+        add(0, 2)
+        mx(0, 3)
         load(RB)
         load(RB + 1)
+        qw(1)
+        add(0, 3)
+        hm(1, EV_HB)
+        th(2, EV_TH)
+        actv(0, 2, 4)
+        widen(3)
+        ti(2, EV_TI)
+        load(2 + RB)
 
         def late(c, half):
             nb = geo(c)[4]
             return range(half * nb // 2, (half + 1) * nb // 2)
 
-        for s in range(NSTEP - 2):
+        for s in range(1, NSTEP - 2):
             c, q = STEPS[s]
             u0, size, nj, tpb, nb = geo(c)
             st[("z", c, q)] = zp.tile([P, T, size], F32, name="z%d" % q, tag="z%d" % q)

@@ -25,11 +25,11 @@ LI = 2
 QPOS = 4
 EV_TH = "ss"
 EV_TI = "ss"
-EV_HB = "v"
-E_IG = "vgvg"
-E_FC = "vgvg"
+EV_HB = "s"
+E_IG = "vvgg"
+E_FC = "vvgg"
 E_C = "gggg"
-E_H = "vgvg"
+E_H = "vvvv"
 T_FC = "vvvv"
 T_C = "vgvg"
 T_H = "vvvv"

@@ -403,6 +403,7 @@ def tile_naivelstm_pa_kernel(
                     actv(s, 0, nb // 2)
             actv(s, nb // 2, nb)
             qw(s + 1)
+            th(s + 2, EV_TH)
             hm(s + 1, EV_HB)
             for cc, h in due:
                 if cc < NCH - 2:
@@ -418,7 +419,6 @@ def tile_naivelstm_pa_kernel(
                     p_fc(c, a + 1, (T_FC if last_f else E_FC)[a + 1])
                     p_c(c, a, (T_C if last_f else E_C)[a])
                     p_c(c, a + 1, (T_C if last_f else E_C)[a + 1])
-            th(s + 2, EV_TH)
             for so in range(NSTEP):
                 if STEPS[so][1] == 3 and s == (so - 3 if so < NSTEP - 2 else so - WEARLY):
                     widen(so)

@@ -37,6 +37,12 @@ T_H2 = "ggvv"
 IDLE = [6, 0]
 F2 = (1, 1)
 R_EV = "ss"
+EVQ = (("ss", "s", "ss"), ("ss", "s", "ss"), ("ss", "s", "ss"), ("vv", "v", "ss"))
+HSPLIT = 4
+AMERGE = False
+TMERGE = True
+VMERGE = False
+S_ORDER = "hb_first"
 WEARLY = 4
 
 
@@ -86,8 +92,10 @@ def tile_naivelstm_pa_kernel(
 
         st = {}
 
-        def evac(eng, out, in_):
-            if eng == "v":
+        def evac(eng, out, in_, later=None):
+            if later is not None:
+                later.append((eng, out, in_))
+            elif eng == "v":
                 nc.vector.tensor_copy(out=out, in_=in_)
             else:
                 nc.scalar.copy(out=out, in_=in_)
@@ -175,7 +183,11 @@ def tile_naivelstm_pa_kernel(
                 in_=st[("xg", tp)][:].rearrange("p a k -> p (a k)"),
             )
 
-        def ti(s, engs, fill=(0, 0)):
+        def flush(later):
+            for eng, out, in_ in later:
+                evac(eng, out, in_)
+
+        def ti(s, engs, fill=(0, 0), later=None):
             if s >= NSTEP:
                 return
             u0, size, nj, tpb, nb = geo(STEPS[s][0])
@@ -187,6 +199,7 @@ def tile_naivelstm_pa_kernel(
                     engs[j],
                     wg[:].bitcast(F32).rearrange("p (g r u) -> p g r u", g=2, u=2)[:, :, j * P:(j + 1) * P, :],
                     tr[:].rearrange("p (g u r) -> p g r u", g=2, u=2),
+                    later,
                 )
 
         def qw(s):
@@ -217,7 +230,7 @@ def tile_naivelstm_pa_kernel(
                 trb = bf_transposes(h0_sb)
                 evac("s", h0T[:].rearrange("p k b -> p (k b)"), trb[:])
 
-        def th(s, engs, fill=(0, 0)):
+        def th(s, engs, fill=(0, 0), later=None):
             if s >= NSTEP:
                 return
             u0, size, nj, tpb, nb = geo(STEPS[s][0])
@@ -229,28 +242,32 @@ def tile_naivelstm_pa_kernel(
             for j in range(nj):
                 if WORDS_H:
                     tr = word_transposes(st[("wh_raw", s)][:, j, :], 1, fill[j])
-                    evac(engs[j], whT[:, :, j * P:(j + 1) * P], tr[:].rearrange("p (a r) -> p a r", a=4))
+                    evac(engs[j], whT[:, :, j * P:(j + 1) * P], tr[:].rearrange("p (a r) -> p a r", a=4), later)
                 else:
                     trb = bf_transposes(st[("wh_raw", s)][:, j, :])
                     evac(engs[j], whT[:, :, j * P:(j + 1) * P], trb[:].rearrange("p (k r) -> p k r", k=8))
 
-        def hm(s, eng):
+        def hm(s, eng, later=None, part=None):
             if s >= NSTEP:
                 return
             c, q = STEPS[s]
             u0, size, nj, tpb, nb = geo(c)
-            hb_ps = psum.tile([P, size], F32, name="hb_ps", tag="bank")
+            if part in (None, 0):
+                st[("hb_ps", s)] = psum.tile([P, size], F32, name="hb_ps", tag="bank")
+            hb_ps = st[("hb_ps", s)]
             whT = st[("whT", s)]
-            for k in range(8):
+            for k in (range(8) if part is None else range(HSPLIT) if part == 0 else range(HSPLIT, 8)):
                 if WORDS_H:
                     rhs = whT[:, k // 2, :].bitcast(BF16)[:, k % 2::2]
                 else:
                     rhs = whT[:, k, :]
                 nc.tensor.matmul(out=hb_ps[:], lhsT=h0T[:, k, :], rhs=rhs, start=(k == 0), stop=False)
+            if part == 0:
+                return
             nc.tensor.matmul(out=hb_ps[:], lhsT=ones_b[:], rhs=bias_rows[:, q, u0:u0 + size], start=False, stop=True)
             hb_sb = stage.tile([P, size], F32, name="hb_sb", tag="hb_sb")
             st[("hb", s)] = hb_sb
-            evac(eng, hb_sb[:], hb_ps[:])
+            evac(eng, hb_sb[:], hb_ps[:], later)
 
         def mx(s, b):
             u0, size, nj, tpb, nb = geo(STEPS[s][0])
@@ -271,9 +288,9 @@ def tile_naivelstm_pa_kernel(
                         stop=(g == 1),
                     )
 
-        def piece(c, q, b):
+        def piece(c, q, b, n=1):
             tpb = geo(c)[3]
-            return st[("z", c, q)][:, b * tpb:(b + 1) * tpb, :]
+            return st[("z", c, q)][:, b * tpb:(b + n) * tpb, :]
 
         def add(s, b):
             c, q = STEPS[s]
@@ -297,30 +314,30 @@ def tile_naivelstm_pa_kernel(
             else:
                 nc.gpsimd.tensor_tensor(out=out, in0=in0, in1=in1, op=op)
 
-        def p_ig(c, b, eng):
-            tt_on(eng, piece(c, 0, b), piece(c, 0, b), piece(c, 1, b), ALU.mult)
+        def p_ig(c, b, eng, n=1):
+            tt_on(eng, piece(c, 0, b, n), piece(c, 0, b, n), piece(c, 1, b, n), ALU.mult)
 
-        def p_fc(c, b, eng):
+        def p_fc(c, b, eng, n=1):
             u0, size, nj, tpb, nb = geo(c)
-            tt_on(eng, piece(c, 2, b), piece(c, 2, b),
-                  c0_sb[:, u0:u0 + size].unsqueeze(1).to_broadcast([P, tpb, size]), ALU.mult)
+            tt_on(eng, piece(c, 2, b, n), piece(c, 2, b, n),
+                  c0_sb[:, u0:u0 + size].unsqueeze(1).to_broadcast([P, n * tpb, size]), ALU.mult)
 
-        def p_c(c, b, eng):
+        def p_c(c, b, eng, n=1):
             u0, size, nj, tpb, nb = geo(c)
-            tt_on(eng, piece(c, 2, b), piece(c, 2, b), piece(c, 0, b), ALU.add)
-            if b == nb - 1:
+            tt_on(eng, piece(c, 2, b, n), piece(c, 2, b, n), piece(c, 0, b, n), ALU.add)
+            if b + n == nb:
                 nc.sync.dma_start(out=out_2[0, :, u0:u0 + size], in_=st[("z", c, 2)][:, T - 1, :])
 
-        def tanh_c(c, b):
-            nc.scalar.activation(out=piece(c, 1, b), in_=piece(c, 2, b), func=ACT.Tanh)
+        def tanh_c(c, b, n=1):
+            nc.scalar.activation(out=piece(c, 1, b, n), in_=piece(c, 2, b, n), func=ACT.Tanh)
 
-        def p_h(c, b, eng):
+        def p_h(c, b, eng, n=1):
             u0, size, nj, tpb, nb = geo(c)
-            tt_on(eng, piece(c, 3, b), piece(c, 3, b), piece(c, 1, b), ALU.mult)
+            tt_on(eng, piece(c, 3, b, n), piece(c, 3, b, n), piece(c, 1, b, n), ALU.mult)
             nc.sync.dma_start(
-                out=out_0[b * tpb:(b + 1) * tpb, :, u0:u0 + size].rearrange("t b h -> b t h"), in_=piece(c, 3, b)
+                out=out_0[b * tpb:(b + n) * tpb, :, u0:u0 + size].rearrange("t b h -> b t h"), in_=piece(c, 3, b, n)
             )
-            if b == nb - 1:
+            if b + n == nb:
                 nc.sync.dma_start(out=out_1[0, :, u0:u0 + size], in_=st[("z", c, 3)][:, T - 1, :])
 
         nc.vector.memset(warm[:], 0.0)
@@ -393,36 +410,67 @@ def tile_naivelstm_pa_kernel(
             st[("z", c, q)] = zp.tile([P, T, size], F32, name="z%d" % q, tag="z%d" % q)
             due = [(cc, s - f_at[cc] - 2) for cc in range(NCH) if s - f_at[cc] in (2, 3)]
             for cc, h in due:
-                for b in late(cc, h):
-                    tanh_c(cc, b)
+                if TMERGE:
+                    tanh_c(cc, late(cc, h)[0], len(late(cc, h)))
+                else:
+                    for b in late(cc, h):
+                        tanh_c(cc, b)
             for b in range(nb):
                 mx(s, b)
             for b in range(nb):
                 add(s, b)
-                if b == nb // 2 - 1:
+                if b == nb // 2 - 1 and not AMERGE:
                     actv(s, 0, nb // 2)
-            actv(s, nb // 2, nb)
+            actv(s, 0 if AMERGE else nb // 2, nb)
             qw(s + 1)
-            th(s + 2, EV_TH)
-            hm(s + 1, EV_HB)
+            ev_th, ev_hb = [], []
+            hm(s + 1, EVQ[q][1], ev_hb, 0)
+            th(s + 2, EVQ[q][0], (0, 0), ev_th)
+            hm(s + 1, EVQ[q][1], ev_hb, 1)
+            if S_ORDER == "hb_first":
+                flush(ev_hb)
+                flush(ev_th)
+            elif S_ORDER == "hb_late":
+                flush(ev_th)
+            else:
+                flush(ev_th)
+                flush(ev_hb)
             for cc, h in due:
                 if cc < NCH - 2:
-                    for b in late(cc, h):
-                        p_h(cc, b, E_H[b])
+                    if VMERGE:
+                        p_h(cc, late(cc, h)[0], "v", len(late(cc, h)))
+                    else:
+                        for b in late(cc, h):
+                            p_h(cc, b, E_H[b])
             last_f = s == NSTEP - 3
             if q == 1:
-                for b in range(nb):
-                    p_ig(c, b, E_IG[b])
+                if VMERGE:
+                    p_ig(c, 0, "v", 2)
+                    p_ig(c, 2, "g")
+                    p_ig(c, 3, "g")
+                else:
+                    for b in range(nb):
+                        p_ig(c, b, E_IG[b])
             if q == 2:
-                for a in range(0, nb, 2):
-                    p_fc(c, a, (T_FC if last_f else E_FC)[a])
-                    p_fc(c, a + 1, (T_FC if last_f else E_FC)[a + 1])
-                    p_c(c, a, (T_C if last_f else E_C)[a])
-                    p_c(c, a + 1, (T_C if last_f else E_C)[a + 1])
+                if VMERGE and not last_f:
+                    p_fc(c, 0, "v", 2)
+                    p_c(c, 0, "v", 2)
+                    p_fc(c, 2, "g")
+                    p_fc(c, 3, "g")
+                    p_c(c, 2, "g")
+                    p_c(c, 3, "g")
+                else:
+                    for a in range(0, nb, 2):
+                        p_fc(c, a, (T_FC if last_f else E_FC)[a])
+                        p_fc(c, a + 1, (T_FC if last_f else E_FC)[a + 1])
+                        p_c(c, a, (T_C if last_f else E_C)[a])
+                        p_c(c, a + 1, (T_C if last_f else E_C)[a + 1])
+            if S_ORDER == "hb_late":
+                flush(ev_hb)
             for so in range(NSTEP):
                 if STEPS[so][1] == 3 and s == (so - 3 if so < NSTEP - 2 else so - WEARLY):
                     widen(so)
-            ti(s + 2, EV_TI)
+            ti(s + 2, EVQ[q][2])
             load(s + 2 + RB)
 
         sa, sb = NSTEP - 2, NSTEP - 1
@@ -439,8 +487,11 @@ def tile_naivelstm_pa_kernel(
                 qw(sb)
             actv(sa, b, b + 1)
             if b % 2 == 1:
-                tanh_c(cb, b - 1)
-                tanh_c(cb, b)
+                if TMERGE:
+                    tanh_c(cb, b - 1, 2)
+                else:
+                    tanh_c(cb, b - 1)
+                    tanh_c(cb, b)
             if T_H2[b] == "g":
                 p_h(ca, b, "g")
         for b in range(nb):

@@ -39,6 +39,7 @@ F2 = (1, 1)
 R_EV = "ss"
 EVQ = (("ss", "s", "ss"), ("ss", "s", "ss"), ("ss", "s", "ss"), ("vv", "v", "ss"))
 HSPLIT = 4
+WIDEN_PLAN = {1: (7, 0), 3: (7, 1), 7: (14, 0), 8: (14, 1), 11: (15, 0), 12: (15, 1)}
 AMERGE = False
 TMERGE = True
 VMERGE = False
@@ -125,26 +126,26 @@ def tile_naivelstm_pa_kernel(
             st[("wh_raw", s)] = wh_raw
 
         def load_w(s):
-            if s >= NSTEP:
+            if s >= NSTEP or ("w_raw", s) in st:
                 return
             c, q = STEPS[s]
             u0, size, nj, tpb, nb = geo(c)
             rows = slice(u0, u0 + size)
             if q == 3:
-                wbytes = raw.tile([P, nj, I], U8, name="wbytes", tag="wbytes", bufs=2)
+                wbytes = raw.tile([P, nj, I], U8, name="wbytes", tag="wbytes", bufs=4)
                 nc.sync.dma_start(out=wbytes[:], in_=w_io_bytes[rows, :].rearrange("(j p) k -> p j k", p=P))
                 st[("wbytes", s)] = wbytes
-                w_wide = raw.tile([P, nj, I], BF16, name="w_wide", tag="w_wide", bufs=2)
+                w_wide = raw.tile([P, nj, I], BF16, name="w_wide", tag="w_wide", bufs=4)
                 st[("w_raw", s)] = w_wide
             else:
                 w_raw = raw.tile([P, nj, I], BF16, name="w_raw", tag="w_raw")
                 nc.sync.dma_start(out=w_raw[:], in_=w_in[q][rows, :].rearrange("(j p) k -> p j k", p=P))
                 st[("w_raw", s)] = w_raw
 
-        def widen(s):
+        def widen(s, js=(0, 1)):
             if s >= NSTEP:
                 return
-            for j in range(geo(STEPS[s][0])[2]):
+            for j in js:
                 nc.vector.tensor_tensor(
                     out=st[("w_raw", s)][:, j, :],
                     in0=st[("wbytes", s)][:, j, :].bitcast(FP8),
@@ -360,6 +361,9 @@ def tile_naivelstm_pa_kernel(
         nc.sync.dma_start(out=scale_bc[:], in_=w_io_scale.rearrange("o k -> (o k)").partition_broadcast(P))
         load(3)
         load_bias(3)
+        for so in range(NSTEP):
+            if STEPS[so][1] == 3:
+                load_w(so)
         nc.sync.dma_start(out=c0_sb[:], in_=c0[0])
         for s in range(4, RB):
             load(s)
@@ -424,9 +428,10 @@ def tile_naivelstm_pa_kernel(
             actv(s, 0 if AMERGE else nb // 2, nb)
             qw(s + 1)
             ev_th, ev_hb = [], []
-            hm(s + 1, EVQ[q][1], ev_hb, 0)
-            th(s + 2, EVQ[q][0], (0, 0), ev_th)
-            hm(s + 1, EVQ[q][1], ev_hb, 1)
+            busy_s = any(s + 1 - f_at[cc] in (2, 3) for cc in range(NCH))
+            hm(s + 1, "s", ev_hb, 0)
+            th(s + 2, "vs" if busy_s else "ss", (0, 0), ev_th)
+            hm(s + 1, "s", ev_hb, 1)
             if S_ORDER == "hb_first":
                 flush(ev_hb)
                 flush(ev_th)
@@ -467,10 +472,9 @@ def tile_naivelstm_pa_kernel(
                         p_c(c, a + 1, (T_C if last_f else E_C)[a + 1])
             if S_ORDER == "hb_late":
                 flush(ev_hb)
-            for so in range(NSTEP):
-                if STEPS[so][1] == 3 and s == (so - 3 if so < NSTEP - 2 else so - WEARLY):
-                    widen(so)
-            ti(s + 2, EVQ[q][2])
+            if s in WIDEN_PLAN:
+                widen(WIDEN_PLAN[s][0], (WIDEN_PLAN[s][1],))
+            ti(s + 2, "ss")
             load(s + 2 + RB)
 
         sa, sb = NSTEP - 2, NSTEP - 1

@@ -29,17 +29,17 @@ EV_HB = "s"
 E_IG = "vvgg"
 E_FC = "vvgg"
 E_C = "gggg"
-E_H = "vvvv"
+E_H = "ggvv"
 T_FC = "vvvv"
-T_C = "vgvg"
+T_C = "vgvv"
 T_H = "vvvv"
 T_H2 = "ggvv"
 IDLE = [6, 0]
-F2 = (1, 1)
+F2 = (1, 0)
 R_EV = "ss"
 EVQ = (("ss", "s", "ss"), ("ss", "s", "ss"), ("ss", "s", "ss"), ("vv", "v", "ss"))
 HSPLIT = 4
-WIDEN_PLAN = {1: (7, 0), 3: (7, 1), 7: (14, 0), 8: (14, 1), 11: (15, 0), 12: (15, 1)}
+WIDEN_PLAN = {1: (7, 0), 3: (7, 1), 6: (14, 0), 7: (15, 0), 8: (14, 1), 11: (15, 1)}
 AMERGE = False
 TMERGE = True
 VMERGE = False
@@ -487,7 +487,7 @@ def tile_naivelstm_pa_kernel(
         hm(sb, "s")
         for b in range(nb):
             add(sa, b)
-            if b == 0:
+            if b == 1:
                 qw(sb)
             actv(sa, b, b + 1)
             if b % 2 == 1:

@@ -88,8 +88,8 @@ def tile_naivelstm_pa_kernel(
         h0_sb = const.tile([P, H], BF16, name="h0_sb")
         c0_sb = const.tile([P, H], BF16, name="c0_sb")
         h0T = const.tile([P, 8, P], BF16, name="h0T")
-        x_codes = const.tile([P, T, 2 * P], U32, name="x_codes", align_bytes=64)
-        x_scales = const.tile([P, T, 2 * P], U8, name="x_scales", align_bytes=64)
+        x_codes = const.tile([P, T, 2 * P], U32, name="x_codes", align_bytes=256)
+        x_scales = const.tile([P, T, 2 * P], U8, name="x_scales", align_bytes=256)
 
         st = {}
 
@@ -207,8 +207,8 @@ def tile_naivelstm_pa_kernel(
             if s >= NSTEP:
                 return
             size = geo(STEPS[s][0])[1]
-            w_codes = stage.tile([P, 2 * size], U32, name="w_codes", tag="w_codes", align_bytes=64)
-            w_scales = stage.tile([P, 2 * size], U8, name="w_scales", tag="w_scales", align_bytes=64)
+            w_codes = stage.tile([P, 2 * size], U32, name="w_codes", tag="w_codes", align_bytes=256)
+            w_scales = stage.tile([P, 2 * size], U8, name="w_scales", tag="w_scales", align_bytes=256)
             st[("w_codes", s)] = w_codes
             st[("w_scales", s)] = w_scales
             nc.vector.quantize_mx(out=w_codes[:].bitcast(FP8X4), scales=w_scales[:], in_=st[("wg", s)][:])

@@ -33,13 +33,13 @@ E_H = "ggvv"
 T_FC = "vvvv"
 T_C = "vgvv"
 T_H = "vvvv"
-T_H2 = "ggvv"
+T_H2 = "gggv"
 IDLE = [6, 0]
 F2 = (1, 0)
 R_EV = "ss"
 EVQ = (("ss", "s", "ss"), ("ss", "s", "ss"), ("ss", "s", "ss"), ("vv", "v", "ss"))
 HSPLIT = 4
-WIDEN_PLAN = {1: (7, 0), 3: (7, 1), 6: (14, 0), 7: (15, 0), 8: (14, 1), 11: (15, 1)}
+WIDEN_PLAN = {2: (7, 0), 3: (7, 1), 4: (14, 0), 7: (14, 1), 8: (15, 0), 11: (15, 1)}
 AMERGE = False
 TMERGE = True
 VMERGE = False
@@ -346,7 +346,7 @@ def tile_naivelstm_pa_kernel(
         nc.vector.memset(ones_b[:], 1.0)
         nc.vector.memset(zeros_b[:], 0.0)
         make_identity(nc, ident_f[:])
-        nc.vector.memset(bias_rows[:], 0.0)
+        nc.vector.memset(bias_rows[:].rearrange("p q h -> p (q h)").bitcast(U32), 0)
         load_w(0)
         nc.sync.dma_start(out=x_sb[:, 0:2, :], in_=inputs[:, 0:2, :])
         nc.sync.dma_start(out=h0_sb[:], in_=h0[0])

@@ -358,8 +358,9 @@ def tile_naivelstm_pa_kernel(
         load_bias(1)
         load(2)
         load_bias(2)
+        load_w(3)
         nc.sync.dma_start(out=scale_bc[:], in_=w_io_scale.rearrange("o k -> (o k)").partition_broadcast(P))
-        load(3)
+        load_wh(3)
         load_bias(3)
         for so in range(NSTEP):
             if STEPS[so][1] == 3:

from contextlib import ExitStack

import concourse.mybir as mybir
from concourse.masks import make_identity

F32 = mybir.dt.float32
BF16 = mybir.dt.bfloat16
U32 = mybir.dt.uint32
U8 = mybir.dt.uint8
FP8 = mybir.dt.float8_e4m3fn
FP8X4 = mybir.dt.float8_e4m3fn_x4
ACT = mybir.ActivationFunctionType
ALU = mybir.AluOpType

B, T, I, H = 128, 8, 1024, 1024
P = 128
FLOPS = 2 * B * T * I * 4 * H + 2 * B * H * 4 * H

SIZES = [256, 256, 256, 256]
WORDS_H = True
RB = 5
ORDER_A = False
RAMPMIX = False
LI = 2
QPOS = 4
EV_TH = "ss"
EV_TI = "ss"
EV_HB = "s"
E_IG = "vvgg"
E_FC = "vvgg"
E_C = "gggg"
E_H = "ggvv"
T_FC = "vvvv"
T_C = "vgvv"
T_H = "vvvv"
T_H2 = "gggv"
IDLE = [6, 0]
F2 = (1, 0)
R_EV = "ss"
EVQ = (("ss", "s", "ss"), ("ss", "s", "ss"), ("ss", "s", "ss"), ("vv", "v", "ss"))
HSPLIT = 4
WIDEN_PLAN = {2: (7, 0), 3: (7, 1), 4: (14, 0), 7: (14, 1), 8: (15, 0), 11: (15, 1)}
AMERGE = False
TMERGE = True
VMERGE = False
S_ORDER = "hb_first"
WEARLY = 4


def tile_naivelstm_pa_kernel(
    tc, inputs, h0, c0, w_ii, b_ii, w_hi, b_hi, w_if_, b_if_, w_hf, b_hf,
    w_io_bytes, w_io_scale, b_io, w_ho, b_ho, w_ig, b_ig, w_hg, b_hg,
    out_0, out_1, out_2,
):
    nc = tc.nc
    w_in = [w_ii, w_ig, w_if_, None]
    w_hid = [w_hi, w_hg, w_hf, w_ho]
    b_in = [b_ii, b_ig, b_if_, b_io]
    b_hid = [b_hi, b_hg, b_hf, b_ho]
    funcs = [ACT.Sigmoid, ACT.Tanh, ACT.Sigmoid, ACT.Sigmoid]
    starts = [sum(SIZES[:i]) for i in range(len(SIZES))]
    NCH = len(SIZES)
    NSTEP = 4 * NCH
    STEPS = [(c, q) for c in range(NCH - 2) for q in range(4)]
    STEPS += [(c, q) for c in (NCH - 2, NCH - 1) for q in range(3)] + [(NCH - 2, 3), (NCH - 1, 3)]
    f_at = dict((c, STEPS.index((c, 2))) for c in range(NCH))

    def geo(c):
        size = SIZES[c]
        return starts[c], size, size // P, 512 // size, T * size // 512

    with ExitStack() as ctx:
        ctx.enter_context(tc.manual_schedule())
        const = ctx.enter_context(tc.tile_pool(name="const", bufs=1))
        raw = ctx.enter_context(tc.tile_pool(name="raw", bufs=RB))
        stage = ctx.enter_context(tc.tile_pool(name="stage", bufs=3))
        zp = ctx.enter_context(tc.tile_pool(name="zp", bufs=2))
        psum = ctx.enter_context(tc.psum_pool(name="psum", bufs=8))

        ident_f = const.tile([P, P], F32, name="ident_f")
        ident_b = const.tile([P, P], BF16, name="ident_b")
        ones_b = const.tile([P, P], BF16, name="ones_b")
        zeros_b = const.tile([P, 512], BF16, name="zeros_b")
        warm = const.tile([P, 1], F32, name="warm")
        bias_rows = const.tile([P, 4, H], BF16, name="bias_rows")
        scale_bc = const.tile([P, I], F32, name="scale_bc")
        x_sb = const.tile([P, T, I], BF16, name="x_sb")
        h0_sb = const.tile([P, H], BF16, name="h0_sb")
        c0_sb = const.tile([P, H], BF16, name="c0_sb")
        h0T = const.tile([P, 8, P], BF16, name="h0T")
        x_codes = const.tile([P, T, 2 * P], U32, name="x_codes", align_bytes=256)
        x_scales = const.tile([P, T, 2 * P], U8, name="x_scales", align_bytes=256)

        st = {}

        def evac(eng, out, in_, later=None):
            if later is not None:
                later.append((eng, out, in_))
            elif eng == "v":
                nc.vector.tensor_copy(out=out, in_=in_)
            else:
                nc.scalar.copy(out=out, in_=in_)

        def load(s):
            load_wh(s)
            load_w(s)

        def load_bias(q):
            nc.sync.dma_start(out=bias_rows[0:1, q, :], in_=b_in[q].rearrange("n o -> o n"))
            nc.sync.dma_start(out=bias_rows[1:2, q, :], in_=b_hid[q].rearrange("n o -> o n"))

        def idle(n):
            if n:
                idle_ps = psum.tile([P, 512], F32, name="idle_ps", tag="bank")
                for i in range(n):
                    nc.tensor.matmul(out=idle_ps[:], lhsT=ones_b[:], rhs=zeros_b[:], start=True, stop=True)

        def load_wh(s):
            if s >= NSTEP:
                return
            c, q = STEPS[s]
            u0, size, nj, tpb, nb = geo(c)
            rows = slice(u0, u0 + size)
            wh_raw = raw.tile([P, nj, H], BF16, name="wh_raw", tag="wh_raw")
            nc.sync.dma_start(out=wh_raw[:], in_=w_hid[q][rows, :].rearrange("(j p) k -> p j k", p=P))
            st[("wh_raw", s)] = wh_raw

        def load_w(s):
            if s >= NSTEP or ("w_raw", s) in st:
                return
            c, q = STEPS[s]
            u0, size, nj, tpb, nb = geo(c)
            rows = slice(u0, u0 + size)
            if q == 3:
                wbytes = raw.tile([P, nj, I], U8, name="wbytes", tag="wbytes", bufs=4)
                nc.sync.dma_start(out=wbytes[:], in_=w_io_bytes[rows, :].rearrange("(j p) k -> p j k", p=P))
                st[("wbytes", s)] = wbytes
                w_wide = raw.tile([P, nj, I], BF16, name="w_wide", tag="w_wide", bufs=4)
                st[("w_raw", s)] = w_wide
            else:
                w_raw = raw.tile([P, nj, I], BF16, name="w_raw", tag="w_raw")
                nc.sync.dma_start(out=w_raw[:], in_=w_in[q][rows, :].rearrange("(j p) k -> p j k", p=P))
                st[("w_raw", s)] = w_raw

        def widen(s, js=(0, 1)):
            if s >= NSTEP:
                return
            for j in js:
                nc.vector.tensor_tensor(
                    out=st[("w_raw", s)][:, j, :],
                    in0=st[("wbytes", s)][:, j, :].bitcast(FP8),
                    in1=scale_bc[:],
                    op=ALU.mult,
                )

        def word_transposes(src_row, step, fill=0):
            words = src_row.bitcast(F32)
            tr = psum.tile([P, 512], F32, name="tr", tag="bank")
            for i in range(fill):
                nc.tensor.matmul(out=tr[:], lhsT=ones_b[:], rhs=zeros_b[:], start=True, stop=True)
            for a in range(4):
                if step == 2:
                    src = words[:, 256 * (a // 2) + a % 2:256 * (a // 2 + 1):2]
                else:
                    src = words[:, a * P:(a + 1) * P]
                nc.tensor.transpose(tr[:, a * P:(a + 1) * P], src, ident_f[:])
            return tr

        def tx(tp, engs, fill=(0, 0)):
            xg = stage.tile([P, 2, 1024], BF16, name="xg", tag="grp", align_bytes=64)
            st[("xg", tp)] = xg
            for tt in range(2):
                tr = word_transposes(x_sb[:, 2 * tp + tt, :], 2, fill[tt])
                evac(
                    engs[tt],
                    xg[:, tt, :].bitcast(F32).rearrange("p (g b u) -> p g b u", g=2, u=2),
                    tr[:].rearrange("p (g u b) -> p g b u", g=2, u=2),
                )

        def qx(tp):
            nc.vector.quantize_mx(
                out=x_codes[:, 2 * tp:2 * tp + 2, :].rearrange("p t w -> p (t w)").bitcast(FP8X4),
                scales=x_scales[:, 2 * tp:2 * tp + 2, :].rearrange("p t w -> p (t w)"),
                in_=st[("xg", tp)][:].rearrange("p a k -> p (a k)"),
            )

        def flush(later):
            for eng, out, in_ in later:
                evac(eng, out, in_)

        def ti(s, engs, fill=(0, 0), later=None):
            if s >= NSTEP:
                return
            u0, size, nj, tpb, nb = geo(STEPS[s][0])
            wg = stage.tile([P, 8 * size], BF16, name="wg", tag="grp", align_bytes=64)
            st[("wg", s)] = wg
            for j in range(nj):
                tr = word_transposes(st[("w_raw", s)][:, j, :], 2, fill[j])
                evac(
                    engs[j],
                    wg[:].bitcast(F32).rearrange("p (g r u) -> p g r u", g=2, u=2)[:, :, j * P:(j + 1) * P, :],
                    tr[:].rearrange("p (g u r) -> p g r u", g=2, u=2),
                    later,
                )

        def qw(s):
            if s >= NSTEP:
                return
            size = geo(STEPS[s][0])[1]
            w_codes = stage.tile([P, 2 * size], U32, name="w_codes", tag="w_codes", align_bytes=256)
            w_scales = stage.tile([P, 2 * size], U8, name="w_scales", tag="w_scales", align_bytes=256)
            st[("w_codes", s)] = w_codes
            st[("w_scales", s)] = w_scales
            nc.vector.quantize_mx(out=w_codes[:].bitcast(FP8X4), scales=w_scales[:], in_=st[("wg", s)][:])

        def bf_transposes(src_row):
            trb = psum.tile([P, 1024], BF16, name="trb", tag="bank")
            for k in range(8):
                nc.tensor.transpose(trb[:, k * P:(k + 1) * P], src_row[:, k * P:(k + 1) * P], ident_b[:])
            return trb

        def th0(fill=0):
            if WORDS_H:
                tr = word_transposes(h0_sb, 1, fill)
                evac(
                    "s",
                    h0T[:].rearrange("p (a e) b -> p a e b", e=2),
                    tr[:].bitcast(BF16).rearrange("p (a b e) -> p a e b", a=4, e=2),
                )
            else:
                trb = bf_transposes(h0_sb)
                evac("s", h0T[:].rearrange("p k b -> p (k b)"), trb[:])

        def th(s, engs, fill=(0, 0), later=None):
            if s >= NSTEP:
                return
            u0, size, nj, tpb, nb = geo(STEPS[s][0])
            if WORDS_H:
                whT = stage.tile([P, 4, size], F32, name="whT", tag="whT")
            else:
                whT = stage.tile([P, 8, size], BF16, name="whT", tag="whT")
            st[("whT", s)] = whT
            for j in range(nj):
                if WORDS_H:
                    tr = word_transposes(st[("wh_raw", s)][:, j, :], 1, fill[j])
                    evac(engs[j], whT[:, :, j * P:(j + 1) * P], tr[:].rearrange("p (a r) -> p a r", a=4), later)
                else:
                    trb = bf_transposes(st[("wh_raw", s)][:, j, :])
                    evac(engs[j], whT[:, :, j * P:(j + 1) * P], trb[:].rearrange("p (k r) -> p k r", k=8))

        def hm(s, eng, later=None, part=None):
            if s >= NSTEP:
                return
            c, q = STEPS[s]
            u0, size, nj, tpb, nb = geo(c)
            if part in (None, 0):
                st[("hb_ps", s)] = psum.tile([P, size], F32, name="hb_ps", tag="bank")
            hb_ps = st[("hb_ps", s)]
            whT = st[("whT", s)]
            for k in (range(8) if part is None else range(HSPLIT) if part == 0 else range(HSPLIT, 8)):
                if WORDS_H:
                    rhs = whT[:, k // 2, :].bitcast(BF16)[:, k % 2::2]
                else:
                    rhs = whT[:, k, :]
                nc.tensor.matmul(out=hb_ps[:], lhsT=h0T[:, k, :], rhs=rhs, start=(k == 0), stop=False)
            if part == 0:
                return
            nc.tensor.matmul(out=hb_ps[:], lhsT=ones_b[:], rhs=bias_rows[:, q, u0:u0 + size], start=False, stop=True)
            hb_sb = stage.tile([P, size], F32, name="hb_sb", tag="hb_sb")
            st[("hb", s)] = hb_sb
            evac(eng, hb_sb[:], hb_ps[:], later)

        def mx(s, b):
            u0, size, nj, tpb, nb = geo(STEPS[s][0])
            acc = psum.tile([P, tpb, size], F32, name="acc", tag="bank")
            st[("acc", s, b)] = acc
            w_codes = st[("w_codes", s)]
            w_scales = st[("w_scales", s)]
            for tt in range(tpb):
                t = tpb * b + tt
                for g in range(2):
                    nc.tensor.matmul_mx(
                        out=acc[:, tt, :],
                        lhsT=x_codes[:, t, g * P:(g + 1) * P].bitcast(FP8X4),
                        lhsT_scale=x_scales[:, t, g * P:(g + 1) * P],
                        rhs=w_codes[:, g * size:(g + 1) * size].bitcast(FP8X4),
                        rhs_scale=w_scales[:, g * size:(g + 1) * size],
                        start=(g == 0),
                        stop=(g == 1),
                    )

        def piece(c, q, b, n=1):
            tpb = geo(c)[3]
            return st[("z", c, q)][:, b * tpb:(b + n) * tpb, :]

        def add(s, b):
            c, q = STEPS[s]
            u0, size, nj, tpb, nb = geo(c)
            nc.vector.tensor_tensor(
                out=piece(c, q, b),
                in0=st[("acc", s, b)][:],
                in1=st[("hb", s)][:].unsqueeze(1).to_broadcast([P, tpb, size]),
                op=ALU.add,
            )

        def actv(s, b0, b1):
            c, q = STEPS[s]
            tpb = geo(c)[3]
            z = st[("z", c, q)][:, b0 * tpb:b1 * tpb, :]
            nc.scalar.activation(out=z, in_=z, func=funcs[q])

        def tt_on(eng, out, in0, in1, op):
            if eng == "v":
                nc.vector.tensor_tensor(out=out, in0=in0, in1=in1, op=op)
            else:
                nc.gpsimd.tensor_tensor(out=out, in0=in0, in1=in1, op=op)

        def p_ig(c, b, eng, n=1):
            tt_on(eng, piece(c, 0, b, n), piece(c, 0, b, n), piece(c, 1, b, n), ALU.mult)

        def p_fc(c, b, eng, n=1):
            u0, size, nj, tpb, nb = geo(c)
            tt_on(eng, piece(c, 2, b, n), piece(c, 2, b, n),
                  c0_sb[:, u0:u0 + size].unsqueeze(1).to_broadcast([P, n * tpb, size]), ALU.mult)

        def p_c(c, b, eng, n=1):
            u0, size, nj, tpb, nb = geo(c)
            tt_on(eng, piece(c, 2, b, n), piece(c, 2, b, n), piece(c, 0, b, n), ALU.add)
            if b + n == nb:
                nc.sync.dma_start(out=out_2[0, :, u0:u0 + size], in_=st[("z", c, 2)][:, T - 1, :])

        def tanh_c(c, b, n=1):
            nc.scalar.activation(out=piece(c, 1, b, n), in_=piece(c, 2, b, n), func=ACT.Tanh)

        def p_h(c, b, eng, n=1):
            u0, size, nj, tpb, nb = geo(c)
            tt_on(eng, piece(c, 3, b, n), piece(c, 3, b, n), piece(c, 1, b, n), ALU.mult)
            nc.sync.dma_start(
                out=out_0[b * tpb:(b + n) * tpb, :, u0:u0 + size].rearrange("t b h -> b t h"), in_=piece(c, 3, b, n)
            )
            if b + n == nb:
                nc.sync.dma_start(out=out_1[0, :, u0:u0 + size], in_=st[("z", c, 3)][:, T - 1, :])

        nc.vector.memset(warm[:], 0.0)
        nc.scalar.activation(out=warm[:], in_=warm[:], func=ACT.Sigmoid)
        nc.vector.memset(ones_b[:], 1.0)
        nc.vector.memset(zeros_b[:], 0.0)
        make_identity(nc, ident_f[:])
        nc.vector.memset(bias_rows[:].rearrange("p q h -> p (q h)").bitcast(U32), 0)
        load_w(0)
        nc.sync.dma_start(out=x_sb[:, 0:2, :], in_=inputs[:, 0:2, :])
        nc.sync.dma_start(out=h0_sb[:], in_=h0[0])
        load_wh(0)
        load_bias(0)
        for tp in range(1, 4):
            nc.sync.dma_start(out=x_sb[:, 2 * tp:2 * tp + 2, :], in_=inputs[:, 2 * tp:2 * tp + 2, :])
        load(1)
        load_bias(1)
        load(2)
        load_bias(2)
        load_w(3)
        nc.sync.dma_start(out=scale_bc[:], in_=w_io_scale.rearrange("o k -> (o k)").partition_broadcast(P))
        load_wh(3)
        load_bias(3)
        for so in range(NSTEP):
            if STEPS[so][1] == 3:
                load_w(so)
        nc.sync.dma_start(out=c0_sb[:], in_=c0[0])
        for s in range(4, RB):
            load(s)

        st[("z", 0, 0)] = zp.tile([P, T, SIZES[0]], F32, name="z0", tag="z0")
        idle(IDLE[0])
        ti(0, "vs", F2)
        tx(0, "ss", F2)
        qw(0)
        th0(F2[0])
        th(0, "vs", F2)
        qx(0)
        tx(1, "vs", F2)
        mx(0, 0)
        tx(2, "ss")
        qx(1)
        hm(0, "v")
        tx(3, "vs")
        add(0, 0)
        mx(0, 1)
        qx(2)
        th(1, "ss")
        add(0, 1)
        mx(0, 2)
        qx(3)
        actv(0, 0, 2)
        ti(1, "vs")
        add(0, 2)
        mx(0, 3)
        load(RB)
        load(RB + 1)
        qw(1)
        add(0, 3)
        hm(1, EV_HB)
        th(2, EV_TH)
        actv(0, 2, 4)
        widen(3)
        ti(2, EV_TI)
        load(2 + RB)

        def late(c, half):
            nb = geo(c)[4]
            return range(half * nb // 2, (half + 1) * nb // 2)

        for s in range(1, NSTEP - 2):
            c, q = STEPS[s]
            u0, size, nj, tpb, nb = geo(c)
            st[("z", c, q)] = zp.tile([P, T, size], F32, name="z%d" % q, tag="z%d" % q)
            due = [(cc, s - f_at[cc] - 2) for cc in range(NCH) if s - f_at[cc] in (2, 3)]
            for cc, h in due:
                if TMERGE:
                    tanh_c(cc, late(cc, h)[0], len(late(cc, h)))
                else:
                    for b in late(cc, h):
                        tanh_c(cc, b)
            for b in range(nb):
                mx(s, b)
            for b in range(nb):
                add(s, b)
                if b == nb // 2 - 1 and not AMERGE:
                    actv(s, 0, nb // 2)
            actv(s, 0 if AMERGE else nb // 2, nb)
            qw(s + 1)
            ev_th, ev_hb = [], []
            busy_s = any(s + 1 - f_at[cc] in (2, 3) for cc in range(NCH))
            hm(s + 1, "s", ev_hb, 0)
            th(s + 2, "vs" if busy_s else "ss", (0, 0), ev_th)
            hm(s + 1, "s", ev_hb, 1)
            if S_ORDER == "hb_first":
                flush(ev_hb)
                flush(ev_th)
            elif S_ORDER == "hb_late":
                flush(ev_th)
            else:
                flush(ev_th)
                flush(ev_hb)
            for cc, h in due:
                if cc < NCH - 2:
                    if VMERGE:
                        p_h(cc, late(cc, h)[0], "v", len(late(cc, h)))
                    else:
                        for b in late(cc, h):
                            p_h(cc, b, E_H[b])
            last_f = s == NSTEP - 3
            if q == 1:
                if VMERGE:
                    p_ig(c, 0, "v", 2)
                    p_ig(c, 2, "g")
                    p_ig(c, 3, "g")
                else:
                    for b in range(nb):
                        p_ig(c, b, E_IG[b])
            if q == 2:
                if VMERGE and not last_f:
                    p_fc(c, 0, "v", 2)
                    p_c(c, 0, "v", 2)
                    p_fc(c, 2, "g")
                    p_fc(c, 3, "g")
                    p_c(c, 2, "g")
                    p_c(c, 3, "g")
                else:
                    for a in range(0, nb, 2):
                        p_fc(c, a, (T_FC if last_f else E_FC)[a])
                        p_fc(c, a + 1, (T_FC if last_f else E_FC)[a + 1])
                        p_c(c, a, (T_C if last_f else E_C)[a])
                        p_c(c, a + 1, (T_C if last_f else E_C)[a + 1])
            if S_ORDER == "hb_late":
                flush(ev_hb)
            if s in WIDEN_PLAN:
                widen(WIDEN_PLAN[s][0], (WIDEN_PLAN[s][1],))
            ti(s + 2, "ss")
            load(s + 2 + RB)

        sa, sb = NSTEP - 2, NSTEP - 1
        ca, cb = NCH - 2, NCH - 1
        nb = geo(cb)[4]
        for s in (sa, sb):
            st[("z", STEPS[s][0], 3)] = zp.tile([P, T, geo(STEPS[s][0])[1]], F32, name="z3", tag="z3")
        for b in range(nb):
            mx(sa, b)
        hm(sb, "s")
        for b in range(nb):
            add(sa, b)
            if b == 1:
                qw(sb)
            actv(sa, b, b + 1)
            if b % 2 == 1:
                if TMERGE:
                    tanh_c(cb, b - 1, 2)
                else:
                    tanh_c(cb, b - 1)
                    tanh_c(cb, b)
            if T_H2[b] == "g":
                p_h(ca, b, "g")
        for b in range(nb):
            mx(sb, b)
        for b in range(nb):
            add(sb, b)
            actv(sb, b, b + 1)
            if T_H2[b] == "v":
                p_h(ca, b, "v")
        for b in range(nb):
            p_h(cb, b, T_H[b])
